import numpy as np
import ml_dtypes


def mxq(x, axis, fmt="e4m3"):
    dtype, down = {"e4m3": (ml_dtypes.float8_e4m3fn, 7), "e5m2": (ml_dtypes.float8_e5m2, 14)}[fmt]
    v = np.moveaxis(np.asarray(x, np.float32).astype(ml_dtypes.bfloat16).astype(np.float64), axis, -1)
    blocks = v.reshape(v.shape[:-1] + (-1, 32))
    amax = np.abs(blocks).max(-1, keepdims=True)
    byte = np.maximum(np.where(amax > 0, np.frexp(amax)[1] - 1 + 127, 0) - down, 1)
    scale = np.exp2(byte - 127.0)
    codes = (blocks / scale).astype(np.float32).astype(dtype).astype(np.float64)
    return np.moveaxis((codes * scale).reshape(v.shape), -1, axis)


WIDE = False


def mx_kscale(k):
    if not WIDE:
        return np.ones(k)
    levels = np.array([10, -10, 5, -5, 0])
    a = np.random.permutation(np.resize(levels, k // 512 * 4)).reshape(k // 512, 4)
    idx = np.arange(k)
    return np.exp2(a[idx // 512, idx % 128 // 32])


BF16 = ml_dtypes.bfloat16


def bf(x):
    return np.asarray(x, np.float32).astype(BF16)


def f64(x):
    return np.asarray(x).astype(np.float64)


E2M1 = np.array([0.0, 0.5, 1.0, 1.5, 2.0, 3.0, 4.0, 6.0, -0.0, -0.5, -1.0, -1.5, -2.0, -3.0, -4.0, -6.0])


def pack_weight(w, fmt):
    k, n = w.shape
    w = f64(bf(w)).reshape(k // 32, 32, n)
    amax = np.abs(w).max(1)
    if fmt == "e4m3":
        byte = np.frexp(amax)[1] - 1 + 127 - 7
    else:
        mant, ex = np.frexp(amax / 6.0)
        byte = np.where(mant > 0.5, ex, ex - 1) + 127
    byte = np.clip(np.where(amax > 0, byte, 1), 1, 254)
    scaled = (w * np.exp2(127.0 - byte)[:, None, :]).reshape(k, n).astype(np.float32)
    by_word = np.ascontiguousarray(scaled.reshape(k // 512, 128, 4, n).transpose(0, 1, 3, 2))
    if fmt == "e4m3":
        words = by_word.astype(ml_dtypes.float8_e4m3fn).view(np.uint8)
    else:
        c = by_word.astype(ml_dtypes.float4_e2m1fn).view(np.uint8) & 0xF
        words = c[..., 0::2] | (c[..., 1::2] << 4)
    return np.ascontiguousarray(words), np.ascontiguousarray(byte.astype(np.uint8).reshape(k // 512, 16, n))


def unpack_weight(words, scales, fmt):
    g, p, n, _ = words.shape
    if fmt == "e4m3":
        vals = np.ascontiguousarray(words).view(ml_dtypes.float8_e4m3fn).astype(np.float64)
    else:
        nib = np.empty((g, p, n, 4), np.uint8)
        nib[..., 0::2] = words & 0xF
        nib[..., 1::2] = words >> 4
        vals = E2M1[nib]
    vals = vals * np.repeat(np.exp2(scales.astype(np.float64) - 127.0), 8, axis=1)[..., None]
    return vals.transpose(0, 1, 3, 2).reshape(g * 512, n)


B, HD, NH, H, W, F = 2, 1024, 8, 16, 32, 2048
HEAD = HD // NH
P = H * W


def rms_in(x, w, eps=1e-8):
    std = np.std(x, axis=(-2, -1), keepdims=True, ddof=1)
    return x / (std + eps) * w[None, :, None, None]


def setup_inputs():
    n = np.random.standard_normal
    s = mx_kscale(HD)

    def stream():
        return n((B, NH, H, W, HEAD)) * 0.35 * (0.5 + np.random.random((B, NH, 1, 1, HEAD))) + 0.5 * n((B, NH, 1, 1, HEAD))

    xx = bf(stream())
    xy = bf(stream())
    x = bf(n((B, HD, H, W)) * (0.5 + np.random.random((B, HD, 1, 1))) + 0.5 * n((B, HD, 1, 1)))
    norm2_w = bf((1.0 + 0.1 * n(HD)) * s)
    out_w = n((HD, HD)) / np.sqrt(HD) / s[None, :]
    out_w_words, out_w_scales = pack_weight(np.ascontiguousarray(out_w.T), "e4m3")
    out_b = bf(0.1 * n(HD))
    gamma_att = bf(0.5 + 0.2 * n(HD))
    return {"xx": xx, "xy": xy,
            "x": x,
            "norm2_w": norm2_w,
            "out_w_words": out_w_words, "out_w_scales": out_w_scales,
            "out_b": out_b,
            "gamma_att": gamma_att}


def reference(xx, xy, x, norm2_w, out_w_words, out_w_scales, out_b, gamma_att):
    a = (f64(xx) + f64(xy)) * 0.5
    a = a.transpose(0, 1, 4, 2, 3).reshape(B, HD, H, W)
    a = rms_in(a, f64(norm2_w)).reshape(B, HD, P)
    a = (unpack_weight(out_w_words, out_w_scales, "e4m3").T @ mxq(a, 1, "e4m3")) + f64(out_b)[None, :, None]
    return a.reshape(B, HD, H, W) * f64(gamma_att)[None, :, None, None] + f64(x)

@@ -1,0 +1,240 @@
+from contextlib import ExitStack
+
+import concourse.mybir as mybir
+from concourse.masks import make_identity
+
+F32 = mybir.dt.float32
+BF16 = mybir.dt.bfloat16
+I32 = mybir.dt.int32
+U32 = mybir.dt.uint32
+U8 = mybir.dt.uint8
+FP8X4 = mybir.dt.float8_e4m3fn_x4
+ACT = mybir.ActivationFunctionType
+ALU = mybir.AluOpType
+
+P = 128
+PACK = 4
+K_PASS = P * PACK
+BATCH = 2
+HEADS = 8
+HEAD_CH = 128
+CHANNELS = HEADS * HEAD_CH
+POSITIONS = 512
+GROUPS = CHANNELS // K_PASS
+GROUP_HEADS = K_PASS // HEAD_CH
+POS_PER_PART = POSITIONS // P
+HEAD_PARTS = HEAD_CH // PACK
+OUT_TILES = CHANNELS // P
+SCALE_ROWS = 4
+EPS = 1e-8
+
+FLOPS = 2 * BATCH * CHANNELS * CHANNELS * POSITIONS
+
+
+def tile_axialattentionblock_pb_kernel(
+    tc, xx, xy, x, norm2_w, out_w_words, out_w_scales, out_b, gamma_att, out
+):
+    nc = tc.nc
+    units = [(b, g) for b in range(BATCH) for g in range(GROUPS)]
+
+    with ExitStack() as ctx:
+        consts = ctx.enter_context(tc.tile_pool(name="consts", bufs=1))
+        per_unit = ctx.enter_context(tc.tile_pool(name="per_unit", bufs=len(units)))
+        per_batch = ctx.enter_context(tc.tile_pool(name="per_batch", bufs=BATCH))
+        results = ctx.enter_context(tc.tile_pool(name="results", bufs=4))
+        psum = ctx.enter_context(tc.psum_pool(name="psum", bufs=8))
+        ctx.enter_context(tc.manual_schedule())
+
+        ident = consts.tile([P, P], F32)
+        make_identity(nc, ident[:])
+        ident_bf = consts.tile([P, P], BF16)
+        make_identity(nc, ident_bf[:])
+
+        w_planes = consts.tile([P, GROUPS, CHANNELS], U8, align_bytes=64)
+        nc.vector.memset(w_planes[:].bitcast(I32), 0)
+
+        vec_rows = consts.tile([P, P], BF16)
+        nc.vector.memset(vec_rows[:], 0.0)
+        nc.scalar.dma_start(out=vec_rows[0:OUT_TILES, :], in_=gamma_att.rearrange("(m p) -> m p", p=P))
+        nc.scalar.dma_start(out=vec_rows[OUT_TILES : 2 * OUT_TILES, :], in_=out_b.rearrange("(m p) -> m p", p=P))
+        norm_w = consts.tile([P, GROUPS, PACK], BF16)
+        nc.scalar.dma_start(out=norm_w[:], in_=norm2_w.rearrange("(g p t) -> p g t", g=GROUPS, t=PACK))
+
+        one = consts.tile([P, 1], F32)
+        nc.vector.memset(one[:], 1.0)
+        warm = consts.tile([P, 1], F32)
+        nc.scalar.activation(out=warm[:], in_=one[:], func=ACT.Sqrt)
+
+        xx_sb = []
+        xy_sb = []
+        for b, g in units:
+            xx_u = per_unit.tile([P, GROUP_HEADS, POS_PER_PART * HEAD_CH], BF16)
+            xy_u = per_unit.tile([P, GROUP_HEADS, POS_PER_PART * HEAD_CH], BF16)
+            for h in range(GROUP_HEADS):
+                for stream, tile_u in ((xx, xx_u), (xy, xy_u)):
+                    nc.sync.dma_start(
+                        out=tile_u[:, h, :],
+                        in_=stream[b, g * GROUP_HEADS + h].rearrange("y (w i) c -> (y w) (i c)", i=POS_PER_PART),
+                    )
+            xx_sb.append(xx_u)
+            xy_sb.append(xy_u)
+
+        w_words = consts.tile([P, GROUPS, CHANNELS], U32, align_bytes=64)
+        nc.sync.dma_start(
+            out=w_words[:].bitcast(I32),
+            in_=out_w_words.rearrange("g p o t -> p g (o t)").bitcast(I32),
+        )
+        scale_rows = out_w_scales.rearrange("g (q r) o -> r q g o", r=SCALE_ROWS)
+        for r in range(SCALE_ROWS):
+            nc.sync.dma_start(out=w_planes[r:P:32, :, :].bitcast(I32), in_=scale_rows[r].bitcast(I32))
+
+        x_sb = []
+        for b in range(BATCH):
+            x_b = per_batch.tile([P, OUT_TILES, POSITIONS], BF16)
+            x_view = x[b].rearrange("(m p) y w -> p m (y w)", p=P)
+            for half in (slice(0, OUT_TILES // 2), slice(OUT_TILES // 2, OUT_TILES)):
+                nc.sync.dma_start(out=x_b[:, half, :], in_=x_view[:, half, :])
+            x_sb.append(x_b)
+
+        gamma = consts.tile([P, OUT_TILES], F32)
+        bias = consts.tile([P, OUT_TILES], F32)
+        gamma_bias = consts.tile([P, OUT_TILES], F32)
+        half_w = consts.tile([P, GROUPS, PACK], F32)
+        x_bias = [per_batch.tile([P, OUT_TILES, POSITIONS], F32, name="x_bias") for b in range(BATCH)]
+        summed = [per_unit.tile([P, POS_PER_PART, PACK, P], F32, name="summed") for u in units]
+        banks = [[] for u in units]
+        stats = [per_unit.tile([P, PACK, 6], F32, name="stats") for u in units]
+        mean_var = [per_unit.tile([P, PACK, 2], F32, name="mean_var") for u in units]
+        std = [per_unit.tile([P, PACK], F32, name="std") for u in units]
+        factor = [per_unit.tile([P, PACK], F32, name="factor") for u in units]
+        planes = [per_unit.tile([P, PACK, POSITIONS], BF16, name="planes") for u in units]
+        grouped = [per_unit.tile([P, POSITIONS, PACK], BF16, name="grouped", align_bytes=64) for u in units]
+        g_words = [per_unit.tile([P, POSITIONS], U32, name="g_words", align_bytes=64) for u in units]
+        g_planes = [per_unit.tile([P, POSITIONS], U8, name="g_planes", align_bytes=64) for u in units]
+
+        def spread_vectors():
+            vec_cols = psum.tile([P, P], BF16, tag="bank")
+            nc.tensor.transpose(vec_cols[:], vec_rows[:], ident_bf[:])
+            nc.vector.tensor_copy(out=gamma[:], in_=vec_cols[:, 0:OUT_TILES])
+            nc.vector.tensor_copy(out=bias[:], in_=vec_cols[:, OUT_TILES : 2 * OUT_TILES])
+            nc.vector.tensor_mul(out=gamma_bias[:], in0=gamma[:], in1=bias[:])
+            nc.vector.tensor_scalar_mul(out=half_w[:], in0=norm_w[:], scalar1=0.5)
+
+        def add_bias_to_residual(b):
+            for m in range(OUT_TILES):
+                nc.gpsimd.tensor_scalar(
+                    out=x_bias[b][:, m, :],
+                    in0=x_sb[b][:, m, :],
+                    scalar1=1.0,
+                    scalar2=gamma_bias[:, m : m + 1],
+                    op0=ALU.mult,
+                    op1=ALU.add,
+                )
+
+        def add_streams(u, heads):
+            for h in heads:
+                nc.vector.tensor_tensor(
+                    out=summed[u][:, :, :, h * HEAD_PARTS : (h + 1) * HEAD_PARTS],
+                    in0=xx_sb[u][:, h, :].rearrange("q (i c t) -> q i t c", i=POS_PER_PART, t=PACK),
+                    in1=xy_sb[u][:, h, :].rearrange("q (i c t) -> q i t c", i=POS_PER_PART, t=PACK),
+                    op=ALU.add,
+                )
+
+        def transpose_unit(u):
+            for t in range(PACK):
+                bank = psum.tile([P, POSITIONS], F32, tag="bank")
+                for i in range(POS_PER_PART):
+                    nc.tensor.transpose(bank[:, i * P : (i + 1) * P], summed[u][:, i, t, :], ident[:])
+                banks[u].append(bank)
+
+        def deviations(u):
+            for t in range(PACK):
+                nc.vector.bn_stats(out=stats[u][:, t, :], in_=banks[u][t][:])
+                nc.vector.bn_aggr(out=mean_var[u][:, t, :], in_=stats[u][:, t, :])
+            nc.scalar.activation(
+                out=std[u][:], in_=mean_var[u][:, :, 1], func=ACT.Sqrt, scale=0.25 * POSITIONS / (POSITIONS - 1)
+            )
+
+        def factors(u):
+            g = units[u][1]
+            nc.vector.tensor_scalar_add(out=factor[u][:], in0=std[u][:], scalar1=EPS)
+            nc.vector.reciprocal(out=factor[u][:], in_=factor[u][:])
+            nc.vector.tensor_mul(out=factor[u][:], in0=factor[u][:], in1=half_w[:, g, :])
+
+        def scale_unit(u):
+            for t in range(PACK):
+                nc.scalar.activation(
+                    out=planes[u][:, t, :].rearrange("p (q i) -> p q i", i=POS_PER_PART),
+                    in_=banks[u][t][:].rearrange("p (i q) -> p q i", i=POS_PER_PART),
+                    func=ACT.Copy,
+                    scale=factor[u][:, t : t + 1],
+                )
+
+        def regroup_unit(u, cols):
+            nc.scalar.copy(
+                out=grouped[u][:, cols, :].rearrange("p (c i) t -> p c t i", i=4),
+                in_=planes[u][:, :, cols].rearrange("p t (c i) -> p c t i", i=4),
+            )
+
+        def quantise_unit(u):
+            nc.vector.quantize_mx(
+                out=g_words[u][:].bitcast(FP8X4),
+                scales=g_planes[u][:],
+                in_=grouped[u][:].rearrange("p n t -> p (n t)"),
+            )
+
+        def project(b):
+            out_view = out[b].rearrange("(m p) y w -> p m (y w)", p=P)
+            for m in range(OUT_TILES):
+                o_cols = slice(m * P, (m + 1) * P)
+                acc = psum.tile([P, POSITIONS], F32, tag="bank")
+                for g in range(GROUPS):
+                    u = b * GROUPS + g
+                    nc.tensor.matmul_mx(
+                        out=acc[:],
+                        lhsT=w_words[:, g, o_cols].bitcast(FP8X4),
+                        lhsT_scale=w_planes[:, g, o_cols],
+                        rhs=g_words[u][:].bitcast(FP8X4),
+                        rhs_scale=g_planes[u][:],
+                        start=(g == 0),
+                        stop=(g == GROUPS - 1),
+                    )
+                res = results.tile([P, POSITIONS], F32)
+                nc.vector.scalar_tensor_tensor(
+                    out=res[:],
+                    in0=acc[:],
+                    scalar=gamma[:, m : m + 1],
+                    in1=x_bias[b][:, m, :],
+                    op0=ALU.mult,
+                    op1=ALU.add,
+                )
+                nc.sync.dma_start(out=out_view[:, m, :], in_=res[:])
+
+        n_units = len(units)
+        all_heads = range(GROUP_HEADS)
+        first_half = slice(0, POSITIONS // 2)
+        second_half = slice(POSITIONS // 2, POSITIONS)
+
+        add_streams(0, all_heads)
+        transpose_unit(0)
+        spread_vectors()
+        for b in range(BATCH):
+            add_bias_to_residual(b)
+        for u in range(n_units):
+            deviations(u)
+            if u > 0:
+                regroup_unit(u - 1, second_half)
+            if u + 1 < n_units:
+                add_streams(u + 1, all_heads[:1])
+            factors(u)
+            scale_unit(u)
+            if u + 1 < n_units:
+                add_streams(u + 1, all_heads[1:])
+                transpose_unit(u + 1)
+            if u > 0:
+                quantise_unit(u - 1)
+            regroup_unit(u, first_half)
+        regroup_unit(n_units - 1, second_half)
+        project(0)
+        quantise_unit(n_units - 1)
+        project(1)

@@ -27,6 +27,7 @@ HEAD_PARTS = HEAD_CH // PACK
 OUT_TILES = CHANNELS // P
 SCALE_ROWS = 4
 EPS = 1e-8
+AHEAD = 2
 
 FLOPS = 2 * BATCH * CHANNELS * CHANNELS * POSITIONS
 
@@ -41,7 +42,7 @@ def tile_axialattentionblock_pb_kernel(
         consts = ctx.enter_context(tc.tile_pool(name="consts", bufs=1))
         per_unit = ctx.enter_context(tc.tile_pool(name="per_unit", bufs=len(units)))
         per_batch = ctx.enter_context(tc.tile_pool(name="per_batch", bufs=BATCH))
-        results = ctx.enter_context(tc.tile_pool(name="results", bufs=4))
+        results = ctx.enter_context(tc.tile_pool(name="results", bufs=BATCH * OUT_TILES))
         psum = ctx.enter_context(tc.psum_pool(name="psum", bufs=8))
         ctx.enter_context(tc.manual_schedule())
 
@@ -112,9 +113,10 @@ def tile_axialattentionblock_pb_kernel(
         g_words = [per_unit.tile([P, POSITIONS], U32, name="g_words", align_bytes=64) for u in units]
         g_planes = [per_unit.tile([P, POSITIONS], U8, name="g_planes", align_bytes=64) for u in units]
 
+        vec_cols = psum.tile([P, P], BF16, tag="bank")
+        nc.tensor.transpose(vec_cols[:], vec_rows[:], ident_bf[:])
+
         def spread_vectors():
-            vec_cols = psum.tile([P, P], BF16, tag="bank")
-            nc.tensor.transpose(vec_cols[:], vec_rows[:], ident_bf[:])
             nc.vector.tensor_copy(out=gamma[:], in_=vec_cols[:, 0:OUT_TILES])
             nc.vector.tensor_copy(out=bias[:], in_=vec_cols[:, OUT_TILES : 2 * OUT_TILES])
             nc.vector.tensor_mul(out=gamma_bias[:], in0=gamma[:], in1=bias[:])
@@ -150,6 +152,7 @@ def tile_axialattentionblock_pb_kernel(
         def deviations(u):
             for t in range(PACK):
                 nc.vector.bn_stats(out=stats[u][:, t, :], in_=banks[u][t][:])
+            for t in range(PACK):
                 nc.vector.bn_aggr(out=mean_var[u][:, t, :], in_=stats[u][:, t, :])
             nc.scalar.activation(
                 out=std[u][:], in_=mean_var[u][:, :, 1], func=ACT.Sqrt, scale=0.25 * POSITIONS / (POSITIONS - 1)
@@ -220,21 +223,24 @@ def tile_axialattentionblock_pb_kernel(
         spread_vectors()
         for b in range(BATCH):
             add_bias_to_residual(b)
+        add_streams(1, all_heads)
+        transpose_unit(1)
         for u in range(n_units):
             deviations(u)
             if u > 0:
                 regroup_unit(u - 1, second_half)
-            if u + 1 < n_units:
-                add_streams(u + 1, all_heads[:1])
+            if u + AHEAD < n_units:
+                add_streams(u + AHEAD, all_heads[:2])
+            else:
+                quantise_unit(u - AHEAD)
             factors(u)
             scale_unit(u)
-            if u + 1 < n_units:
-                add_streams(u + 1, all_heads[1:])
-                transpose_unit(u + 1)
-            if u > 0:
-                quantise_unit(u - 1)
+            if u + AHEAD < n_units:
+                add_streams(u + AHEAD, all_heads[2:])
+                transpose_unit(u + AHEAD)
             regroup_unit(u, first_half)
         regroup_unit(n_units - 1, second_half)
         project(0)
+        quantise_unit(n_units - 2)
         quantise_unit(n_units - 1)
         project(1)

@@ -27,6 +27,7 @@ HEAD_PARTS = HEAD_CH // PACK
 OUT_TILES = CHANNELS // P
 SCALE_ROWS = 4
 EPS = 1e-8
+LOAD_HEADS = 2
 AHEAD = 2
 
 FLOPS = 2 * BATCH * CHANNELS * CHANNELS * POSITIONS
@@ -71,11 +72,14 @@ def tile_axialattentionblock_pb_kernel(
         for b, g in units:
             xx_u = per_unit.tile([P, GROUP_HEADS, POS_PER_PART * HEAD_CH], BF16)
             xy_u = per_unit.tile([P, GROUP_HEADS, POS_PER_PART * HEAD_CH], BF16)
-            for h in range(GROUP_HEADS):
+            for h in range(0, GROUP_HEADS, LOAD_HEADS):
                 for stream, tile_u in ((xx, xx_u), (xy, xy_u)):
+                    first = g * GROUP_HEADS + h
                     nc.sync.dma_start(
-                        out=tile_u[:, h, :],
-                        in_=stream[b, g * GROUP_HEADS + h].rearrange("y (w i) c -> (y w) (i c)", i=POS_PER_PART),
+                        out=tile_u[:, h : h + LOAD_HEADS, :],
+                        in_=stream[b, first : first + LOAD_HEADS].rearrange(
+                            "n y (w i) c -> (y w) n (i c)", i=POS_PER_PART
+                        ),
                     )
             xx_sb.append(xx_u)
             xy_sb.append(xy_u)

@@ -105,12 +105,14 @@ def tile_axialattentionblock_pb_kernel(
         bias = consts.tile([P, OUT_TILES], F32)
         gamma_bias = consts.tile([P, OUT_TILES], F32)
         half_w = consts.tile([P, GROUPS, PACK], F32)
+        two_over_w = consts.tile([P, GROUPS, PACK], F32)
         x_bias = [per_batch.tile([P, OUT_TILES, POSITIONS], F32, name="x_bias") for b in range(BATCH)]
         summed = [per_unit.tile([P, POS_PER_PART, PACK, P], F32, name="summed") for u in units]
         banks = [[] for u in units]
         stats = [per_unit.tile([P, PACK, 6], F32, name="stats") for u in units]
         mean_var = [per_unit.tile([P, PACK, 2], F32, name="mean_var") for u in units]
         std = [per_unit.tile([P, PACK], F32, name="std") for u in units]
+        divisor = [per_unit.tile([P, PACK], F32, name="divisor") for u in units]
         factor = [per_unit.tile([P, PACK], F32, name="factor") for u in units]
         planes = [per_unit.tile([P, PACK, POSITIONS], BF16, name="planes") for u in units]
         grouped = [per_unit.tile([P, POSITIONS, PACK], BF16, name="grouped", align_bytes=64) for u in units]
@@ -125,6 +127,7 @@ def tile_axialattentionblock_pb_kernel(
             nc.vector.tensor_copy(out=bias[:], in_=vec_cols[:, OUT_TILES : 2 * OUT_TILES])
             nc.vector.tensor_mul(out=gamma_bias[:], in0=gamma[:], in1=bias[:])
             nc.vector.tensor_scalar_mul(out=half_w[:], in0=norm_w[:], scalar1=0.5)
+            nc.vector.reciprocal(out=two_over_w[:], in_=half_w[:])
 
         def add_bias_to_residual(b):
             for m in range(OUT_TILES):
@@ -137,9 +140,9 @@ def tile_axialattentionblock_pb_kernel(
                     op1=ALU.add,
                 )
 
-        def add_streams(u, heads):
+        def add_streams(engine, u, heads):
             for h in heads:
-                nc.vector.tensor_tensor(
+                engine.tensor_tensor(
                     out=summed[u][:, :, :, h * HEAD_PARTS : (h + 1) * HEAD_PARTS],
                     in0=xx_sb[u][:, h, :].rearrange("q (i c t) -> q i t c", i=POS_PER_PART, t=PACK),
                     in1=xy_sb[u][:, h, :].rearrange("q (i c t) -> q i t c", i=POS_PER_PART, t=PACK),
@@ -164,9 +167,10 @@ def tile_axialattentionblock_pb_kernel(
 
         def factors(u):
             g = units[u][1]
-            nc.vector.tensor_scalar_add(out=factor[u][:], in0=std[u][:], scalar1=EPS)
-            nc.vector.reciprocal(out=factor[u][:], in_=factor[u][:])
-            nc.vector.tensor_mul(out=factor[u][:], in0=factor[u][:], in1=half_w[:, g, :])
+            nc.vector.scalar_tensor_tensor(
+                out=divisor[u][:], in0=std[u][:], scalar=EPS, in1=two_over_w[:, g, :], op0=ALU.add, op1=ALU.mult
+            )
+            nc.vector.reciprocal(out=factor[u][:], in_=divisor[u][:])
 
         def scale_unit(u):
             for t in range(PACK):
@@ -177,8 +181,8 @@ def tile_axialattentionblock_pb_kernel(
                     scale=factor[u][:, t : t + 1],
                 )
 
-        def regroup_unit(u, cols):
-            nc.scalar.copy(
+        def regroup_unit(copy, u, cols):
+            copy(
                 out=grouped[u][:, cols, :].rearrange("p (c i) t -> p c t i", i=4),
                 in_=planes[u][:, :, cols].rearrange("p t (c i) -> p c t i", i=4),
             )
@@ -190,9 +194,9 @@ def tile_axialattentionblock_pb_kernel(
                 in_=grouped[u][:].rearrange("p n t -> p (n t)"),
             )
 
-        def project(b):
+        def project(b, out_tiles):
             out_view = out[b].rearrange("(m p) y w -> p m (y w)", p=P)
-            for m in range(OUT_TILES):
+            for m in out_tiles:
                 o_cols = slice(m * P, (m + 1) * P)
                 acc = psum.tile([P, POSITIONS], F32, tag="bank")
                 for g in range(GROUPS):
@@ -221,30 +225,35 @@ def tile_axialattentionblock_pb_kernel(
         all_heads = range(GROUP_HEADS)
         first_half = slice(0, POSITIONS // 2)
         second_half = slice(POSITIONS // 2, POSITIONS)
+        all_tiles = range(OUT_TILES)
 
-        add_streams(0, all_heads)
+        for u in range(AHEAD, n_units):
+            add_streams(nc.gpsimd, u, all_heads[:2])
+        add_streams(nc.vector, 0, all_heads)
         transpose_unit(0)
         spread_vectors()
         for b in range(BATCH):
             add_bias_to_residual(b)
-        add_streams(1, all_heads)
+        add_streams(nc.vector, 1, all_heads)
         transpose_unit(1)
+        deviations(0)
         for u in range(n_units):
-            deviations(u)
-            if u > 0:
-                regroup_unit(u - 1, second_half)
             if u + AHEAD < n_units:
-                add_streams(u + AHEAD, all_heads[:2])
+                add_streams(nc.vector, u + AHEAD, all_heads[2:])
             else:
+                regroup_unit(nc.vector.tensor_copy, u - AHEAD, second_half)
                 quantise_unit(u - AHEAD)
             factors(u)
             scale_unit(u)
             if u + AHEAD < n_units:
-                add_streams(u + AHEAD, all_heads[2:])
                 transpose_unit(u + AHEAD)
-            regroup_unit(u, first_half)
-        regroup_unit(n_units - 1, second_half)
-        project(0)
+            if u + 1 < n_units:
+                deviations(u + 1)
+            regroup_unit(nc.scalar.copy, u, first_half)
+        regroup_unit(nc.vector.tensor_copy, n_units - 2, second_half)
         quantise_unit(n_units - 2)
+        project(0, all_tiles[: OUT_TILES // 2])
+        regroup_unit(nc.vector.tensor_copy, n_units - 1, second_half)
         quantise_unit(n_units - 1)
-        project(1)
+        project(0, all_tiles[OUT_TILES // 2 :])
+        project(1, all_tiles)

@@ -242,8 +242,9 @@ def tile_axialattentionblock_pb_kernel(
                 add_streams(nc.vector, u + AHEAD, all_heads[2:])
             else:
                 regroup_unit(nc.vector.tensor_copy, u - AHEAD, second_half)
-                quantise_unit(u - AHEAD)
             factors(u)
+            if u >= AHEAD:
+                quantise_unit(u - AHEAD)
             scale_unit(u)
             if u + AHEAD < n_units:
                 transpose_unit(u + AHEAD)
@@ -251,9 +252,11 @@ def tile_axialattentionblock_pb_kernel(
                 deviations(u + 1)
             regroup_unit(nc.scalar.copy, u, first_half)
         regroup_unit(nc.vector.tensor_copy, n_units - 2, second_half)
+        project(0, all_tiles[:1])
         quantise_unit(n_units - 2)
-        project(0, all_tiles[: OUT_TILES // 2])
+        project(0, all_tiles[1 : OUT_TILES // 2])
         regroup_unit(nc.vector.tensor_copy, n_units - 1, second_half)
+        project(0, all_tiles[OUT_TILES // 2 : OUT_TILES // 2 + 1])
         quantise_unit(n_units - 1)
-        project(0, all_tiles[OUT_TILES // 2 :])
+        project(0, all_tiles[OUT_TILES // 2 + 1 :])
         project(1, all_tiles)

@@ -251,11 +251,12 @@ def tile_axialattentionblock_pb_kernel(
             if u + 1 < n_units:
                 deviations(u + 1)
             regroup_unit(nc.scalar.copy, u, first_half)
+            if u == n_units - 1:
+                regroup_unit(nc.scalar.copy, u, second_half)
         regroup_unit(nc.vector.tensor_copy, n_units - 2, second_half)
         project(0, all_tiles[:1])
         quantise_unit(n_units - 2)
         project(0, all_tiles[1 : OUT_TILES // 2])
-        regroup_unit(nc.vector.tensor_copy, n_units - 1, second_half)
         project(0, all_tiles[OUT_TILES // 2 : OUT_TILES // 2 + 1])
         quantise_unit(n_units - 1)
         project(0, all_tiles[OUT_TILES // 2 + 1 :])

@@ -232,8 +232,7 @@ def tile_axialattentionblock_pb_kernel(
         add_streams(nc.vector, 0, all_heads)
         transpose_unit(0)
         spread_vectors()
-        for b in range(BATCH):
-            add_bias_to_residual(b)
+        add_bias_to_residual(0)
         add_streams(nc.vector, 1, all_heads)
         transpose_unit(1)
         deviations(0)
@@ -253,6 +252,10 @@ def tile_axialattentionblock_pb_kernel(
             regroup_unit(nc.scalar.copy, u, first_half)
             if u == n_units - 1:
                 regroup_unit(nc.scalar.copy, u, second_half)
+                for m in range(OUT_TILES):
+                    nc.scalar.activation(
+                        out=x_bias[1][:, m, :], in_=x_sb[1][:, m, :], func=ACT.Identity, bias=gamma_bias[:, m : m + 1]
+                    )
         regroup_unit(nc.vector.tensor_copy, n_units - 2, second_half)
         project(0, all_tiles[:1])
         quantise_unit(n_units - 2)

@@ -28,7 +28,9 @@ OUT_TILES = CHANNELS // P
 SCALE_ROWS = 4
 EPS = 1e-8
 LOAD_HEADS = 2
-AHEAD = 2
+VECTOR_UNIT = 0
+PAIR_POS = P // 2
+PAIR_RUNS = POSITIONS // PAIR_POS
 
 FLOPS = 2 * BATCH * CHANNELS * CHANNELS * POSITIONS
 
@@ -51,6 +53,8 @@ def tile_axialattentionblock_pb_kernel(
         make_identity(nc, ident[:])
         ident_bf = consts.tile([P, P], BF16)
         make_identity(nc, ident_bf[:])
+        pair_sum = consts.tile([P, PAIR_POS], BF16)
+        nc.gpsimd.tensor_tensor(out=pair_sum[:], in0=ident_bf[:, 0:P:2], in1=ident_bf[:, 1:P:2], op=ALU.add)
 
         w_planes = consts.tile([P, GROUPS, CHANNELS], U8, align_bytes=64)
         nc.vector.memset(w_planes[:].bitcast(I32), 0)
@@ -69,7 +73,21 @@ def tile_axialattentionblock_pb_kernel(
 
         xx_sb = []
         xy_sb = []
-        for b, g in units:
+        pair_sb = []
+        for u, (b, g) in enumerate(units):
+            if u != VECTOR_UNIT:
+                pair_u = per_unit.tile([P, PAIR_RUNS, K_PASS], BF16)
+                for h in range(GROUP_HEADS):
+                    for s, stream in enumerate((xx, xy)):
+                        nc.sync.dma_start(
+                            out=pair_u[s:P:2, :, h * HEAD_CH : (h + 1) * HEAD_CH],
+                            in_=stream[b, g * GROUP_HEADS + h].rearrange("(j y) w c -> (y w) j c", j=PAIR_RUNS),
+                        )
+                pair_sb.append(pair_u)
+                xx_sb.append(None)
+                xy_sb.append(None)
+                continue
+            pair_sb.append(None)
             xx_u = per_unit.tile([P, GROUP_HEADS, POS_PER_PART * HEAD_CH], BF16)
             xy_u = per_unit.tile([P, GROUP_HEADS, POS_PER_PART * HEAD_CH], BF16)
             for h in range(0, GROUP_HEADS, LOAD_HEADS):
@@ -107,7 +125,7 @@ def tile_axialattentionblock_pb_kernel(
         half_w = consts.tile([P, GROUPS, PACK], F32)
         two_over_w = consts.tile([P, GROUPS, PACK], F32)
         x_bias = [per_batch.tile([P, OUT_TILES, POSITIONS], F32, name="x_bias") for b in range(BATCH)]
-        summed = [per_unit.tile([P, POS_PER_PART, PACK, P], F32, name="summed") for u in units]
+        summed = consts.tile([P, POS_PER_PART, PACK, P], F32)
         banks = [[] for u in units]
         stats = [per_unit.tile([P, PACK, 6], F32, name="stats") for u in units]
         mean_var = [per_unit.tile([P, PACK, 2], F32, name="mean_var") for u in units]
@@ -143,7 +161,7 @@ def tile_axialattentionblock_pb_kernel(
         def add_streams(engine, u, heads):
             for h in heads:
                 engine.tensor_tensor(
-                    out=summed[u][:, :, :, h * HEAD_PARTS : (h + 1) * HEAD_PARTS],
+                    out=summed[:, :, :, h * HEAD_PARTS : (h + 1) * HEAD_PARTS],
                     in0=xx_sb[u][:, h, :].rearrange("q (i c t) -> q i t c", i=POS_PER_PART, t=PACK),
                     in1=xy_sb[u][:, h, :].rearrange("q (i c t) -> q i t c", i=POS_PER_PART, t=PACK),
                     op=ALU.add,
@@ -153,12 +171,27 @@ def tile_axialattentionblock_pb_kernel(
             for t in range(PACK):
                 bank = psum.tile([P, POSITIONS], F32, tag="bank")
                 for i in range(POS_PER_PART):
-                    nc.tensor.transpose(bank[:, i * P : (i + 1) * P], summed[u][:, i, t, :], ident[:])
+                    nc.tensor.transpose(bank[:, i * P : (i + 1) * P], summed[:, i, t, :], ident[:])
                 banks[u].append(bank)
 
-        def deviations(u):
+        def sum_unit(u):
             for t in range(PACK):
+                bank = psum.tile([P, POSITIONS], F32, tag="bank")
+                for j in range(PAIR_RUNS):
+                    nc.tensor.matmul(
+                        bank[:, j * PAIR_POS : (j + 1) * PAIR_POS],
+                        lhsT=pair_sb[u][:, j, t:K_PASS:PACK],
+                        rhs=pair_sum[:],
+                        start=True,
+                        stop=True,
+                    )
+                banks[u].append(bank)
+
+        def bank_stats(u, ts):
+            for t in ts:
                 nc.vector.bn_stats(out=stats[u][:, t, :], in_=banks[u][t][:])
+
+        def deviations(u):
             for t in range(PACK):
                 nc.vector.bn_aggr(out=mean_var[u][:, t, :], in_=stats[u][:, t, :])
             nc.scalar.activation(
@@ -174,9 +207,13 @@ def tile_axialattentionblock_pb_kernel(
 
         def scale_unit(u):
             for t in range(PACK):
+                to, bank = planes[u][:, t, :], banks[u][t][:]
+                if u == VECTOR_UNIT:
+                    to = to.rearrange("p (q i) -> p q i", i=POS_PER_PART)
+                    bank = bank.rearrange("p (i q) -> p q i", i=POS_PER_PART)
                 nc.scalar.activation(
-                    out=planes[u][:, t, :].rearrange("p (q i) -> p q i", i=POS_PER_PART),
-                    in_=banks[u][t][:].rearrange("p (i q) -> p q i", i=POS_PER_PART),
+                    out=to,
+                    in_=bank,
                     func=ACT.Copy,
                     scale=factor[u][:, t : t + 1],
                 )
@@ -221,46 +258,59 @@ def tile_axialattentionblock_pb_kernel(
                 )
                 nc.sync.dma_start(out=out_view[:, m, :], in_=res[:])
 
-        n_units = len(units)
         all_heads = range(GROUP_HEADS)
         first_half = slice(0, POSITIONS // 2)
         second_half = slice(POSITIONS // 2, POSITIONS)
         all_tiles = range(OUT_TILES)
 
-        for u in range(AHEAD, n_units):
-            add_streams(nc.gpsimd, u, all_heads[:2])
+        all_t = range(PACK)
+        v_copy = nc.vector.tensor_copy
+        s_copy = nc.scalar.copy
+
         add_streams(nc.vector, 0, all_heads)
         transpose_unit(0)
         spread_vectors()
         add_bias_to_residual(0)
-        add_streams(nc.vector, 1, all_heads)
-        transpose_unit(1)
+        sum_unit(1)
+        bank_stats(0, all_t)
         deviations(0)
-        for u in range(n_units):
-            if u + AHEAD < n_units:
-                add_streams(nc.vector, u + AHEAD, all_heads[2:])
-            else:
-                regroup_unit(nc.vector.tensor_copy, u - AHEAD, second_half)
-            factors(u)
-            if u >= AHEAD:
-                quantise_unit(u - AHEAD)
-            scale_unit(u)
-            if u + AHEAD < n_units:
-                transpose_unit(u + AHEAD)
-            if u + 1 < n_units:
-                deviations(u + 1)
-            regroup_unit(nc.scalar.copy, u, first_half)
-            if u == n_units - 1:
-                regroup_unit(nc.scalar.copy, u, second_half)
-                for m in range(OUT_TILES):
-                    nc.scalar.activation(
-                        out=x_bias[1][:, m, :], in_=x_sb[1][:, m, :], func=ACT.Identity, bias=gamma_bias[:, m : m + 1]
-                    )
-        regroup_unit(nc.vector.tensor_copy, n_units - 2, second_half)
-        project(0, all_tiles[:1])
-        quantise_unit(n_units - 2)
-        project(0, all_tiles[1 : OUT_TILES // 2])
-        project(0, all_tiles[OUT_TILES // 2 : OUT_TILES // 2 + 1])
-        quantise_unit(n_units - 1)
-        project(0, all_tiles[OUT_TILES // 2 + 1 :])
+        bank_stats(1, all_t[:1])
+        factors(0)
+        scale_unit(0)
+        sum_unit(2)
+        bank_stats(1, all_t[1:])
+        deviations(1)
+        bank_stats(2, all_t[:1])
+        factors(1)
+        regroup_unit(v_copy, 0, second_half)
+        regroup_unit(s_copy, 0, first_half)
+        scale_unit(1)
+        sum_unit(3)
+        bank_stats(2, all_t[1:])
+        deviations(2)
+        quantise_unit(0)
+        bank_stats(3, all_t[:1])
+        factors(2)
+        regroup_unit(v_copy, 1, second_half)
+        regroup_unit(s_copy, 1, first_half)
+        scale_unit(2)
+        bank_stats(3, all_t[1:])
+        deviations(3)
+        quantise_unit(1)
+        factors(3)
+        regroup_unit(s_copy, 2, first_half)
+        scale_unit(3)
+        regroup_unit(s_copy, 3, first_half)
+        regroup_unit(s_copy, 3, second_half)
+        for m in range(OUT_TILES):
+            nc.scalar.activation(
+                out=x_bias[1][:, m, :], in_=x_sb[1][:, m, :], func=ACT.Identity, bias=gamma_bias[:, m : m + 1]
+            )
+        project(0, all_tiles[:2])
+        regroup_unit(v_copy, 2, second_half)
+        project(0, all_tiles[2:3])
+        quantise_unit(2)
+        project(0, all_tiles[3:6])
+        quantise_unit(3)
+        project(0, all_tiles[6:])
         project(1, all_tiles)

@@ -45,7 +45,6 @@ def tile_axialattentionblock_pb_kernel(
         consts = ctx.enter_context(tc.tile_pool(name="consts", bufs=1))
         per_unit = ctx.enter_context(tc.tile_pool(name="per_unit", bufs=len(units)))
         per_batch = ctx.enter_context(tc.tile_pool(name="per_batch", bufs=BATCH))
-        results = ctx.enter_context(tc.tile_pool(name="results", bufs=BATCH * OUT_TILES))
         psum = ctx.enter_context(tc.psum_pool(name="psum", bufs=8))
         ctx.enter_context(tc.manual_schedule())
 
@@ -102,22 +101,20 @@ def tile_axialattentionblock_pb_kernel(
             xx_sb.append(xx_u)
             xy_sb.append(xy_u)
 
-        w_words = consts.tile([P, GROUPS, CHANNELS], U32, align_bytes=64)
-        nc.sync.dma_start(
-            out=w_words[:].bitcast(I32),
-            in_=out_w_words.rearrange("g p o t -> p g (o t)").bitcast(I32),
-        )
         scale_rows = out_w_scales.rearrange("g (q r) o -> r q g o", r=SCALE_ROWS)
         for r in range(SCALE_ROWS):
             nc.sync.dma_start(out=w_planes[r:P:32, :, :].bitcast(I32), in_=scale_rows[r].bitcast(I32))
-
-        x_sb = []
-        for b in range(BATCH):
-            x_b = per_batch.tile([P, OUT_TILES, POSITIONS], BF16)
-            x_view = x[b].rearrange("(m p) y w -> p m (y w)", p=P)
-            for half in (slice(0, OUT_TILES // 2), slice(OUT_TILES // 2, OUT_TILES)):
-                nc.sync.dma_start(out=x_b[:, half, :], in_=x_view[:, half, :])
-            x_sb.append(x_b)
+        w_words = consts.tile([P, GROUPS, CHANNELS], U32, align_bytes=64)
+        w_view = out_w_words.rearrange("g p o t -> p g (o t)").bitcast(I32)
+        x_sb = [per_batch.tile([P, OUT_TILES, POSITIONS], BF16, name="x_sb") for b in range(BATCH)]
+        x_view = [x[b].rearrange("(m p) y w -> p m (y w)", p=P) for b in range(BATCH)]
+        halves = (slice(0, OUT_TILES // 2), slice(OUT_TILES // 2, OUT_TILES))
+        for half in halves:
+            o_cols = slice(half.start * P, half.stop * P)
+            nc.sync.dma_start(out=w_words[:, :, o_cols].bitcast(I32), in_=w_view[:, :, o_cols])
+            nc.sync.dma_start(out=x_sb[0][:, half, :], in_=x_view[0][:, half, :])
+        for half in halves:
+            nc.sync.dma_start(out=x_sb[1][:, half, :], in_=x_view[1][:, half, :])
 
         gamma = consts.tile([P, OUT_TILES], F32)
         bias = consts.tile([P, OUT_TILES], F32)
@@ -126,6 +123,7 @@ def tile_axialattentionblock_pb_kernel(
         two_over_w = consts.tile([P, GROUPS, PACK], F32)
         x_bias = [per_batch.tile([P, OUT_TILES, POSITIONS], F32, name="x_bias") for b in range(BATCH)]
         summed = consts.tile([P, POS_PER_PART, PACK, P], F32)
+        res = [per_batch.tile([P, OUT_TILES, POSITIONS], F32, name="res") for b in range(BATCH)]
         banks = [[] for u in units]
         stats = [per_unit.tile([P, PACK, 6], F32, name="stats") for u in units]
         mean_var = [per_unit.tile([P, PACK, 2], F32, name="mean_var") for u in units]
@@ -147,8 +145,8 @@ def tile_axialattentionblock_pb_kernel(
             nc.vector.tensor_scalar_mul(out=half_w[:], in0=norm_w[:], scalar1=0.5)
             nc.vector.reciprocal(out=two_over_w[:], in_=half_w[:])
 
-        def add_bias_to_residual(b):
-            for m in range(OUT_TILES):
+        def add_bias_to_residual(b, out_tiles):
+            for m in out_tiles:
                 nc.gpsimd.tensor_scalar(
                     out=x_bias[b][:, m, :],
                     in0=x_sb[b][:, m, :],
@@ -191,22 +189,29 @@ def tile_axialattentionblock_pb_kernel(
             for t in ts:
                 nc.vector.bn_stats(out=stats[u][:, t, :], in_=banks[u][t][:])
 
-        def deviations(u):
-            for t in range(PACK):
+        def deviations(u, ts):
+            for t in ts:
                 nc.vector.bn_aggr(out=mean_var[u][:, t, :], in_=stats[u][:, t, :])
+            cols = slice(ts[0], ts[-1] + 1)
             nc.scalar.activation(
-                out=std[u][:], in_=mean_var[u][:, :, 1], func=ACT.Sqrt, scale=0.25 * POSITIONS / (POSITIONS - 1)
+                out=std[u][:, cols], in_=mean_var[u][:, cols, 1], func=ACT.Sqrt, scale=0.25 * POSITIONS / (POSITIONS - 1)
             )
 
-        def factors(u):
+        def factors(u, ts):
             g = units[u][1]
+            cols = slice(ts[0], ts[-1] + 1)
             nc.vector.scalar_tensor_tensor(
-                out=divisor[u][:], in0=std[u][:], scalar=EPS, in1=two_over_w[:, g, :], op0=ALU.add, op1=ALU.mult
+                out=divisor[u][:, cols],
+                in0=std[u][:, cols],
+                scalar=EPS,
+                in1=two_over_w[:, g, cols],
+                op0=ALU.add,
+                op1=ALU.mult,
             )
-            nc.vector.reciprocal(out=factor[u][:], in_=divisor[u][:])
+            nc.vector.reciprocal(out=factor[u][:, cols], in_=divisor[u][:, cols])
 
-        def scale_unit(u):
-            for t in range(PACK):
+        def scale_unit(u, ts):
+            for t in ts:
                 to, bank = planes[u][:, t, :], banks[u][t][:]
                 if u == VECTOR_UNIT:
                     to = to.rearrange("p (q i) -> p q i", i=POS_PER_PART)
@@ -224,14 +229,14 @@ def tile_axialattentionblock_pb_kernel(
                 in_=planes[u][:, :, cols].rearrange("p t (c i) -> p c t i", i=4),
             )
 
-        def quantise_unit(u):
+        def quantise_unit(u, cols=slice(0, POSITIONS)):
             nc.vector.quantize_mx(
-                out=g_words[u][:].bitcast(FP8X4),
-                scales=g_planes[u][:],
-                in_=grouped[u][:].rearrange("p n t -> p (n t)"),
+                out=g_words[u][:, cols].bitcast(FP8X4),
+                scales=g_planes[u][:, cols],
+                in_=grouped[u][:, cols, :].rearrange("p n t -> p (n t)"),
             )
 
-        def project(b, out_tiles):
+        def project(b, out_tiles, cols=slice(0, POSITIONS), store_tiles=1):
             out_view = out[b].rearrange("(m p) y w -> p m (y w)", p=P)
             for m in out_tiles:
                 o_cols = slice(m * P, (m + 1) * P)
@@ -239,24 +244,25 @@ def tile_axialattentionblock_pb_kernel(
                 for g in range(GROUPS):
                     u = b * GROUPS + g
                     nc.tensor.matmul_mx(
-                        out=acc[:],
+                        out=acc[:, 0 : cols.stop - cols.start],
                         lhsT=w_words[:, g, o_cols].bitcast(FP8X4),
                         lhsT_scale=w_planes[:, g, o_cols],
-                        rhs=g_words[u][:].bitcast(FP8X4),
-                        rhs_scale=g_planes[u][:],
+                        rhs=g_words[u][:, cols].bitcast(FP8X4),
+                        rhs_scale=g_planes[u][:, cols],
                         start=(g == 0),
                         stop=(g == GROUPS - 1),
                     )
-                res = results.tile([P, POSITIONS], F32)
                 nc.vector.scalar_tensor_tensor(
-                    out=res[:],
-                    in0=acc[:],
+                    out=res[b][:, m, cols],
+                    in0=acc[:, 0 : cols.stop - cols.start],
                     scalar=gamma[:, m : m + 1],
-                    in1=x_bias[b][:, m, :],
+                    in1=x_bias[b][:, m, cols],
                     op0=ALU.mult,
                     op1=ALU.add,
                 )
-                nc.sync.dma_start(out=out_view[:, m, :], in_=res[:])
+                if (m + 1) % store_tiles == 0:
+                    ms = slice(m + 1 - store_tiles, m + 1)
+                    nc.sync.dma_start(out=out_view[:, ms, cols], in_=res[b][:, ms, cols])
 
         all_heads = range(GROUP_HEADS)
         first_half = slice(0, POSITIONS // 2)
@@ -270,47 +276,49 @@ def tile_axialattentionblock_pb_kernel(
         add_streams(nc.vector, 0, all_heads)
         transpose_unit(0)
         spread_vectors()
-        add_bias_to_residual(0)
         sum_unit(1)
-        bank_stats(0, all_t)
-        deviations(0)
+        bank_stats(0, all_t[:2])
+        deviations(0, all_t[:2])
+        bank_stats(0, all_t[2:3])
+        factors(0, all_t[:2])
+        scale_unit(0, all_t[:2])
+        bank_stats(0, all_t[3:])
+        deviations(0, all_t[2:])
         bank_stats(1, all_t[:1])
-        factors(0)
-        scale_unit(0)
+        factors(0, all_t[2:])
+        scale_unit(0, all_t[2:])
         sum_unit(2)
         bank_stats(1, all_t[1:])
-        deviations(1)
-        bank_stats(2, all_t[:1])
-        factors(1)
+        deviations(1, all_t)
         regroup_unit(v_copy, 0, second_half)
+        factors(1, all_t)
         regroup_unit(s_copy, 0, first_half)
-        scale_unit(1)
+        scale_unit(1, all_t)
         sum_unit(3)
-        bank_stats(2, all_t[1:])
-        deviations(2)
-        quantise_unit(0)
-        bank_stats(3, all_t[:1])
-        factors(2)
+        bank_stats(2, all_t)
+        deviations(2, all_t)
         regroup_unit(v_copy, 1, second_half)
+        factors(2, all_t)
         regroup_unit(s_copy, 1, first_half)
-        scale_unit(2)
-        bank_stats(3, all_t[1:])
-        deviations(3)
+        quantise_unit(0)
+        scale_unit(2, all_t)
         quantise_unit(1)
-        factors(3)
         regroup_unit(s_copy, 2, first_half)
-        scale_unit(3)
+        bank_stats(3, all_t)
+        deviations(3, all_t)
+        factors(3, all_t)
+        regroup_unit(s_copy, 2, second_half)
+        add_bias_to_residual(0, all_tiles)
+        scale_unit(3, all_t)
+        project(0, all_tiles[:3])
+        quantise_unit(2)
+        project(0, all_tiles[3:7])
         regroup_unit(s_copy, 3, first_half)
         regroup_unit(s_copy, 3, second_half)
-        for m in range(OUT_TILES):
+        for m in all_tiles[0:]:
             nc.scalar.activation(
                 out=x_bias[1][:, m, :], in_=x_sb[1][:, m, :], func=ACT.Identity, bias=gamma_bias[:, m : m + 1]
             )
-        project(0, all_tiles[:2])
-        regroup_unit(v_copy, 2, second_half)
-        project(0, all_tiles[2:3])
-        quantise_unit(2)
-        project(0, all_tiles[3:6])
         quantise_unit(3)
-        project(0, all_tiles[6:])
+        project(0, all_tiles[7:])
         project(1, all_tiles)

@@ -29,6 +29,7 @@ SCALE_ROWS = 4
 EPS = 1e-8
 LOAD_HEADS = 2
 VECTOR_UNIT = 0
+SORTED_UNIT = 1
 PAIR_POS = P // 2
 PAIR_RUNS = POSITIONS // PAIR_POS
 
@@ -74,6 +75,19 @@ def tile_axialattentionblock_pb_kernel(
         xy_sb = []
         pair_sb = []
         for u, (b, g) in enumerate(units):
+            if u == SORTED_UNIT:
+                raw = consts.tile([P, GROUP_HEADS, PAIR_RUNS * HEAD_CH], BF16)
+                for h in range(0, GROUP_HEADS, LOAD_HEADS):
+                    for s, stream in enumerate((xx, xy)):
+                        first = g * GROUP_HEADS + h
+                        nc.sync.dma_start(
+                            out=raw[s:P:2, h : h + LOAD_HEADS, :],
+                            in_=stream[b, first : first + LOAD_HEADS].rearrange("n y (w j) c -> (y w) n (j c)", j=PAIR_RUNS),
+                        )
+                pair_sb.append(per_unit.tile([P, PAIR_RUNS, K_PASS], BF16, name="pair_u"))
+                xx_sb.append(None)
+                xy_sb.append(None)
+                continue
             if u != VECTOR_UNIT:
                 pair_u = per_unit.tile([P, PAIR_RUNS, K_PASS], BF16)
                 for h in range(GROUP_HEADS):
@@ -172,6 +186,13 @@ def tile_axialattentionblock_pb_kernel(
                     nc.tensor.transpose(bank[:, i * P : (i + 1) * P], summed[:, i, t, :], ident[:])
                 banks[u].append(bank)
 
+        def sort_heads(copy, heads):
+            for h in heads:
+                copy(
+                    out=pair_sb[SORTED_UNIT][:, :, h * HEAD_CH : (h + 1) * HEAD_CH],
+                    in_=raw[:, h, :].rearrange("p (j c) -> p j c", j=PAIR_RUNS),
+                )
+
         def sum_unit(u):
             for t in range(PACK):
                 bank = psum.tile([P, POSITIONS], F32, tag="bank")
@@ -213,6 +234,9 @@ def tile_axialattentionblock_pb_kernel(
         def scale_unit(u, ts):
             for t in ts:
                 to, bank = planes[u][:, t, :], banks[u][t][:]
+                if u == SORTED_UNIT:
+                    to = to.rearrange("p (r j) -> p r j", j=PAIR_RUNS)
+                    bank = bank.rearrange("p (j r) -> p r j", j=PAIR_RUNS)
                 if u == VECTOR_UNIT:
                     to = to.rearrange("p (q i) -> p q i", i=POS_PER_PART)
                     bank = bank.rearrange("p (i q) -> p q i", i=POS_PER_PART)
@@ -228,6 +252,9 @@ def tile_axialattentionblock_pb_kernel(
                 out=grouped[u][:, cols, :].rearrange("p (c i) t -> p c t i", i=4),
                 in_=planes[u][:, :, cols].rearrange("p t (c i) -> p c t i", i=4),
             )
+
+        def g_copy(out, in_):
+            nc.gpsimd.tensor_scalar(out=out, in0=in_, scalar1=1.0, scalar2=0.0, op0=ALU.mult, op1=ALU.add)
 
         def quantise_unit(u, cols=slice(0, POSITIONS)):
             nc.vector.quantize_mx(
@@ -275,6 +302,9 @@ def tile_axialattentionblock_pb_kernel(
 
         add_streams(nc.vector, 0, all_heads)
         transpose_unit(0)
+        sort_heads(v_copy, all_heads[:1])
+        sort_heads(s_copy, all_heads[1:3])
+        sort_heads(g_copy, all_heads[3:])
         spread_vectors()
         sum_unit(1)
         bank_stats(0, all_t[:2])
@@ -290,29 +320,31 @@ def tile_axialattentionblock_pb_kernel(
         sum_unit(2)
         bank_stats(1, all_t[1:])
         deviations(1, all_t)
-        regroup_unit(v_copy, 0, second_half)
+        regroup_unit(g_copy, 0, second_half)
+        bank_stats(2, all_t[:1])
         factors(1, all_t)
         regroup_unit(s_copy, 0, first_half)
         scale_unit(1, all_t)
         sum_unit(3)
-        bank_stats(2, all_t)
+        bank_stats(2, all_t[1:])
         deviations(2, all_t)
-        regroup_unit(v_copy, 1, second_half)
-        factors(2, all_t)
-        regroup_unit(s_copy, 1, first_half)
         quantise_unit(0)
+        factors(2, all_t)
+        regroup_unit(g_copy, 1, second_half)
+        regroup_unit(s_copy, 1, first_half)
         scale_unit(2, all_t)
-        quantise_unit(1)
-        regroup_unit(s_copy, 2, first_half)
         bank_stats(3, all_t)
         deviations(3, all_t)
+        quantise_unit(1)
         factors(3, all_t)
-        regroup_unit(s_copy, 2, second_half)
-        add_bias_to_residual(0, all_tiles)
+        regroup_unit(s_copy, 2, first_half)
+        add_bias_to_residual(0, all_tiles[:3])
+        regroup_unit(g_copy, 2, second_half)
+        add_bias_to_residual(0, all_tiles[3:])
         scale_unit(3, all_t)
-        project(0, all_tiles[:3])
+        project(0, all_tiles[:4])
         quantise_unit(2)
-        project(0, all_tiles[3:7])
+        project(0, all_tiles[4:7])
         regroup_unit(s_copy, 3, first_half)
         regroup_unit(s_copy, 3, second_half)
         for m in all_tiles[0:]:

@@ -253,9 +253,6 @@ def tile_axialattentionblock_pb_kernel(
                 in_=planes[u][:, :, cols].rearrange("p t (c i) -> p c t i", i=4),
             )
 
-        def g_copy(out, in_):
-            nc.gpsimd.tensor_scalar(out=out, in0=in_, scalar1=1.0, scalar2=0.0, op0=ALU.mult, op1=ALU.add)
-
         def quantise_unit(u, cols=slice(0, POSITIONS)):
             nc.vector.quantize_mx(
                 out=g_words[u][:, cols].bitcast(FP8X4),
@@ -299,6 +296,7 @@ def tile_axialattentionblock_pb_kernel(
         all_t = range(PACK)
         v_copy = nc.vector.tensor_copy
         s_copy = nc.scalar.copy
+        g_copy = nc.gpsimd.tensor_copy
 
         add_streams(nc.vector, 0, all_heads)
         transpose_unit(0)

@@ -253,6 +253,11 @@ def tile_axialattentionblock_pb_kernel(
                 in_=planes[u][:, :, cols].rearrange("p t (c i) -> p c t i", i=4),
             )
 
+        def regroup_on_gpsimd(u, cols):
+            nc.gpsimd.tensor_copy(
+                out=grouped[u][:, cols, :], in_=planes[u][:, :, cols].rearrange("p t n -> p n t")
+            )
+
         def quantise_unit(u, cols=slice(0, POSITIONS)):
             nc.vector.quantize_mx(
                 out=g_words[u][:, cols].bitcast(FP8X4),
@@ -296,13 +301,12 @@ def tile_axialattentionblock_pb_kernel(
         all_t = range(PACK)
         v_copy = nc.vector.tensor_copy
         s_copy = nc.scalar.copy
-        g_copy = nc.gpsimd.tensor_copy
 
         add_streams(nc.vector, 0, all_heads)
         transpose_unit(0)
         sort_heads(v_copy, all_heads[:1])
         sort_heads(s_copy, all_heads[1:3])
-        sort_heads(g_copy, all_heads[3:])
+        sort_heads(nc.gpsimd.tensor_copy, all_heads[3:])
         spread_vectors()
         sum_unit(1)
         bank_stats(0, all_t[:2])
@@ -318,7 +322,7 @@ def tile_axialattentionblock_pb_kernel(
         sum_unit(2)
         bank_stats(1, all_t[1:])
         deviations(1, all_t)
-        regroup_unit(g_copy, 0, second_half)
+        regroup_on_gpsimd(0, second_half)
         bank_stats(2, all_t[:1])
         factors(1, all_t)
         regroup_unit(s_copy, 0, first_half)
@@ -328,7 +332,7 @@ def tile_axialattentionblock_pb_kernel(
         deviations(2, all_t)
         quantise_unit(0)
         factors(2, all_t)
-        regroup_unit(g_copy, 1, second_half)
+        regroup_on_gpsimd(1, second_half)
         regroup_unit(s_copy, 1, first_half)
         scale_unit(2, all_t)
         bank_stats(3, all_t)
@@ -337,7 +341,7 @@ def tile_axialattentionblock_pb_kernel(
         factors(3, all_t)
         regroup_unit(s_copy, 2, first_half)
         add_bias_to_residual(0, all_tiles[:3])
-        regroup_unit(g_copy, 2, second_half)
+        regroup_on_gpsimd(2, second_half)
         add_bias_to_residual(0, all_tiles[3:])
         scale_unit(3, all_t)
         project(0, all_tiles[:4])

@@ -29,7 +29,7 @@ SCALE_ROWS = 4
 EPS = 1e-8
 LOAD_HEADS = 2
 VECTOR_UNIT = 0
-SORTED_UNIT = 1
+SORTED_UNITS = (1,)
 PAIR_POS = P // 2
 PAIR_RUNS = POSITIONS // PAIR_POS
 
@@ -45,6 +45,7 @@ def tile_axialattentionblock_pb_kernel(
     with ExitStack() as ctx:
         consts = ctx.enter_context(tc.tile_pool(name="consts", bufs=1))
         per_unit = ctx.enter_context(tc.tile_pool(name="per_unit", bufs=len(units)))
+        streams = ctx.enter_context(tc.tile_pool(name="streams", bufs=1))
         per_batch = ctx.enter_context(tc.tile_pool(name="per_batch", bufs=BATCH))
         psum = ctx.enter_context(tc.psum_pool(name="psum", bufs=8))
         ctx.enter_context(tc.manual_schedule())
@@ -74,9 +75,11 @@ def tile_axialattentionblock_pb_kernel(
         xx_sb = []
         xy_sb = []
         pair_sb = []
+        raw_sb = {}
         for u, (b, g) in enumerate(units):
-            if u == SORTED_UNIT:
-                raw = consts.tile([P, GROUP_HEADS, PAIR_RUNS * HEAD_CH], BF16)
+            if u in SORTED_UNITS:
+                raw = streams.tile([P, GROUP_HEADS, PAIR_RUNS * HEAD_CH], BF16, name="raw_%d" % u)
+                raw_sb[u] = raw
                 for h in range(0, GROUP_HEADS, LOAD_HEADS):
                     for s, stream in enumerate((xx, xy)):
                         first = g * GROUP_HEADS + h
@@ -84,12 +87,12 @@ def tile_axialattentionblock_pb_kernel(
                             out=raw[s:P:2, h : h + LOAD_HEADS, :],
                             in_=stream[b, first : first + LOAD_HEADS].rearrange("n y (w j) c -> (y w) n (j c)", j=PAIR_RUNS),
                         )
-                pair_sb.append(per_unit.tile([P, PAIR_RUNS, K_PASS], BF16, name="pair_u"))
+                pair_sb.append(streams.tile([P, PAIR_RUNS, K_PASS], BF16, name="pair_%d" % u))
                 xx_sb.append(None)
                 xy_sb.append(None)
                 continue
             if u != VECTOR_UNIT:
-                pair_u = per_unit.tile([P, PAIR_RUNS, K_PASS], BF16)
+                pair_u = streams.tile([P, PAIR_RUNS, K_PASS], BF16, name="pair_%d" % u)
                 for h in range(GROUP_HEADS):
                     for s, stream in enumerate((xx, xy)):
                         nc.sync.dma_start(
@@ -101,8 +104,8 @@ def tile_axialattentionblock_pb_kernel(
                 xy_sb.append(None)
                 continue
             pair_sb.append(None)
-            xx_u = per_unit.tile([P, GROUP_HEADS, POS_PER_PART * HEAD_CH], BF16)
-            xy_u = per_unit.tile([P, GROUP_HEADS, POS_PER_PART * HEAD_CH], BF16)
+            xx_u = streams.tile([P, GROUP_HEADS, POS_PER_PART * HEAD_CH], BF16)
+            xy_u = streams.tile([P, GROUP_HEADS, POS_PER_PART * HEAD_CH], BF16)
             for h in range(0, GROUP_HEADS, LOAD_HEADS):
                 for stream, tile_u in ((xx, xx_u), (xy, xy_u)):
                     first = g * GROUP_HEADS + h
@@ -133,8 +136,7 @@ def tile_axialattentionblock_pb_kernel(
         gamma = consts.tile([P, OUT_TILES], F32)
         bias = consts.tile([P, OUT_TILES], F32)
         gamma_bias = consts.tile([P, OUT_TILES], F32)
-        half_w = consts.tile([P, GROUPS, PACK], F32)
-        two_over_w = consts.tile([P, GROUPS, PACK], F32)
+        one_over_w = consts.tile([P, GROUPS, PACK], F32)
         x_bias = [per_batch.tile([P, OUT_TILES, POSITIONS], F32, name="x_bias") for b in range(BATCH)]
         summed = consts.tile([P, POS_PER_PART, PACK, P], F32)
         res = [per_batch.tile([P, OUT_TILES, POSITIONS], F32, name="res") for b in range(BATCH)]
@@ -153,11 +155,9 @@ def tile_axialattentionblock_pb_kernel(
         nc.tensor.transpose(vec_cols[:], vec_rows[:], ident_bf[:])
 
         def spread_vectors():
-            nc.vector.tensor_copy(out=gamma[:], in_=vec_cols[:, 0:OUT_TILES])
-            nc.vector.tensor_copy(out=bias[:], in_=vec_cols[:, OUT_TILES : 2 * OUT_TILES])
-            nc.vector.tensor_mul(out=gamma_bias[:], in0=gamma[:], in1=bias[:])
-            nc.vector.tensor_scalar_mul(out=half_w[:], in0=norm_w[:], scalar1=0.5)
-            nc.vector.reciprocal(out=two_over_w[:], in_=half_w[:])
+            nc.scalar.copy(out=gamma[:], in_=vec_cols[:, 0:OUT_TILES])
+            nc.scalar.copy(out=bias[:], in_=vec_cols[:, OUT_TILES : 2 * OUT_TILES])
+            nc.gpsimd.tensor_tensor(out=gamma_bias[:], in0=gamma[:], in1=bias[:], op=ALU.mult)
 
         def add_bias_to_residual(b, out_tiles):
             for m in out_tiles:
@@ -186,11 +186,14 @@ def tile_axialattentionblock_pb_kernel(
                     nc.tensor.transpose(bank[:, i * P : (i + 1) * P], summed[:, i, t, :], ident[:])
                 banks[u].append(bank)
 
-        def sort_heads(copy, heads):
+        def g_copy(out, in_):
+            nc.gpsimd.tensor_scalar(out=out, in0=in_, scalar1=1.0, scalar2=0.0, op0=ALU.mult, op1=ALU.add)
+
+        def sort_heads(copy, u, heads):
             for h in heads:
                 copy(
-                    out=pair_sb[SORTED_UNIT][:, :, h * HEAD_CH : (h + 1) * HEAD_CH],
-                    in_=raw[:, h, :].rearrange("p (j c) -> p j c", j=PAIR_RUNS),
+                    out=pair_sb[u][:, :, h * HEAD_CH : (h + 1) * HEAD_CH],
+                    in_=raw_sb[u][:, h, :].rearrange("k (j c) -> k j c", j=PAIR_RUNS),
                 )
 
         def sum_unit(u):
@@ -215,26 +218,29 @@ def tile_axialattentionblock_pb_kernel(
                 nc.vector.bn_aggr(out=mean_var[u][:, t, :], in_=stats[u][:, t, :])
             cols = slice(ts[0], ts[-1] + 1)
             nc.scalar.activation(
-                out=std[u][:, cols], in_=mean_var[u][:, cols, 1], func=ACT.Sqrt, scale=0.25 * POSITIONS / (POSITIONS - 1)
+                out=std[u][:, cols], in_=mean_var[u][:, cols, 1], func=ACT.Sqrt, scale=POSITIONS / (POSITIONS - 1)
             )
 
-        def factors(u, ts):
+        def divisors(u, ts):
             g = units[u][1]
             cols = slice(ts[0], ts[-1] + 1)
             nc.vector.scalar_tensor_tensor(
                 out=divisor[u][:, cols],
                 in0=std[u][:, cols],
-                scalar=EPS,
-                in1=two_over_w[:, g, cols],
+                scalar=2.0 * EPS,
+                in1=one_over_w[:, g, cols],
                 op0=ALU.add,
                 op1=ALU.mult,
             )
+
+        def factors(u, ts):
+            cols = slice(ts[0], ts[-1] + 1)
             nc.vector.reciprocal(out=factor[u][:, cols], in_=divisor[u][:, cols])
 
         def scale_unit(u, ts):
             for t in ts:
                 to, bank = planes[u][:, t, :], banks[u][t][:]
-                if u == SORTED_UNIT:
+                if u in SORTED_UNITS:
                     to = to.rearrange("p (r j) -> p r j", j=PAIR_RUNS)
                     bank = bank.rearrange("p (j r) -> p r j", j=PAIR_RUNS)
                 if u == VECTOR_UNIT:
@@ -254,9 +260,7 @@ def tile_axialattentionblock_pb_kernel(
             )
 
         def regroup_on_gpsimd(u, cols):
-            nc.gpsimd.tensor_copy(
-                out=grouped[u][:, cols, :], in_=planes[u][:, :, cols].rearrange("p t n -> p n t")
-            )
+            g_copy(out=grouped[u][:, cols, :], in_=planes[u][:, :, cols].rearrange("p t n -> p n t"))
 
         def quantise_unit(u, cols=slice(0, POSITIONS)):
             nc.vector.quantize_mx(
@@ -302,57 +306,57 @@ def tile_axialattentionblock_pb_kernel(
         v_copy = nc.vector.tensor_copy
         s_copy = nc.scalar.copy
 
+        spread_vectors()
         add_streams(nc.vector, 0, all_heads)
         transpose_unit(0)
-        sort_heads(v_copy, all_heads[:1])
-        sort_heads(s_copy, all_heads[1:3])
-        sort_heads(nc.gpsimd.tensor_copy, all_heads[3:])
-        spread_vectors()
+        sort_heads(v_copy, 1, all_heads[:2])
+        nc.vector.reciprocal(out=one_over_w[:], in_=norm_w[:])
+        sort_heads(v_copy, 1, all_heads[2:])
         sum_unit(1)
-        bank_stats(0, all_t[:2])
-        deviations(0, all_t[:2])
-        bank_stats(0, all_t[2:3])
-        factors(0, all_t[:2])
-        scale_unit(0, all_t[:2])
-        bank_stats(0, all_t[3:])
-        deviations(0, all_t[2:])
+        bank_stats(0, all_t)
+        deviations(0, all_t)
         bank_stats(1, all_t[:1])
-        factors(0, all_t[2:])
-        scale_unit(0, all_t[2:])
+        divisors(0, all_t)
+        bank_stats(1, all_t[1:2])
+        factors(0, all_t)
+        scale_unit(0, all_t)
         sum_unit(2)
-        bank_stats(1, all_t[1:])
+        bank_stats(1, all_t[2:])
         deviations(1, all_t)
-        regroup_on_gpsimd(0, second_half)
-        bank_stats(2, all_t[:1])
-        factors(1, all_t)
         regroup_unit(s_copy, 0, first_half)
+        regroup_on_gpsimd(0, second_half)
+        divisors(1, all_t)
+        factors(1, all_t)
         scale_unit(1, all_t)
         sum_unit(3)
-        bank_stats(2, all_t[1:])
+        bank_stats(2, all_t)
         deviations(2, all_t)
         quantise_unit(0)
-        factors(2, all_t)
-        regroup_on_gpsimd(1, second_half)
         regroup_unit(s_copy, 1, first_half)
+        regroup_on_gpsimd(1, second_half)
+        divisors(2, all_t)
+        bank_stats(3, all_t[:1])
+        factors(2, all_t)
         scale_unit(2, all_t)
-        bank_stats(3, all_t)
-        deviations(3, all_t)
+        bank_stats(3, all_t[1:])
         quantise_unit(1)
-        factors(3, all_t)
+        deviations(3, all_t)
+        add_bias_to_residual(0, all_tiles)
         regroup_unit(s_copy, 2, first_half)
-        add_bias_to_residual(0, all_tiles[:3])
-        regroup_on_gpsimd(2, second_half)
-        add_bias_to_residual(0, all_tiles[3:])
+        regroup_unit(s_copy, 2, second_half)
+        divisors(3, all_t)
+        project(0, all_tiles[:1])
+        factors(3, all_t)
         scale_unit(3, all_t)
-        project(0, all_tiles[:4])
+        project(0, all_tiles[1:4])
         quantise_unit(2)
-        project(0, all_tiles[4:7])
+        project(0, all_tiles[4:6])
         regroup_unit(s_copy, 3, first_half)
-        regroup_unit(s_copy, 3, second_half)
-        for m in all_tiles[0:]:
+        regroup_unit(v_copy, 3, second_half)
+        for m in all_tiles:
             nc.scalar.activation(
                 out=x_bias[1][:, m, :], in_=x_sb[1][:, m, :], func=ACT.Identity, bias=gamma_bias[:, m : m + 1]
             )
         quantise_unit(3)
-        project(0, all_tiles[7:])
+        project(0, all_tiles[6:])
         project(1, all_tiles)

@@ -140,6 +140,7 @@ def tile_axialattentionblock_pb_kernel(
         x_bias = [per_batch.tile([P, OUT_TILES, POSITIONS], F32, name="x_bias") for b in range(BATCH)]
         summed = consts.tile([P, POS_PER_PART, PACK, P], F32)
         res = [per_batch.tile([P, OUT_TILES, POSITIONS], F32, name="res") for b in range(BATCH)]
+        products = [[] for b in range(BATCH)]
         banks = [[] for u in units]
         stats = [per_unit.tile([P, PACK, 6], F32, name="stats") for u in units]
         mean_var = [per_unit.tile([P, PACK, 2], F32, name="mean_var") for u in units]
@@ -269,33 +270,40 @@ def tile_axialattentionblock_pb_kernel(
                 in_=grouped[u][:, cols, :].rearrange("p n t -> p (n t)"),
             )
 
-        def project(b, out_tiles, cols=slice(0, POSITIONS), store_tiles=1):
-            out_view = out[b].rearrange("(m p) y w -> p m (y w)", p=P)
+        def multiply(b, out_tiles, g):
+            u = b * GROUPS + g
             for m in out_tiles:
                 o_cols = slice(m * P, (m + 1) * P)
-                acc = psum.tile([P, POSITIONS], F32, tag="bank")
-                for g in range(GROUPS):
-                    u = b * GROUPS + g
-                    nc.tensor.matmul_mx(
-                        out=acc[:, 0 : cols.stop - cols.start],
-                        lhsT=w_words[:, g, o_cols].bitcast(FP8X4),
-                        lhsT_scale=w_planes[:, g, o_cols],
-                        rhs=g_words[u][:, cols].bitcast(FP8X4),
-                        rhs_scale=g_planes[u][:, cols],
-                        start=(g == 0),
-                        stop=(g == GROUPS - 1),
-                    )
+                if g == 0:
+                    products[b].append(psum.tile([P, POSITIONS], F32, tag="bank", name="product"))
+                nc.tensor.matmul_mx(
+                    out=products[b][m][:],
+                    lhsT=w_words[:, g, o_cols].bitcast(FP8X4),
+                    lhsT_scale=w_planes[:, g, o_cols],
+                    rhs=g_words[u][:].bitcast(FP8X4),
+                    rhs_scale=g_planes[u][:],
+                    start=(g == 0),
+                    stop=(g == GROUPS - 1),
+                )
+
+        def finish(b, out_tiles):
+            out_view = out[b].rearrange("(m p) y w -> p m (y w)", p=P)
+            for m in out_tiles:
                 nc.vector.scalar_tensor_tensor(
-                    out=res[b][:, m, cols],
-                    in0=acc[:, 0 : cols.stop - cols.start],
+                    out=res[b][:, m, :],
+                    in0=products[b][m][:],
                     scalar=gamma[:, m : m + 1],
-                    in1=x_bias[b][:, m, cols],
+                    in1=x_bias[b][:, m, :],
                     op0=ALU.mult,
                     op1=ALU.add,
                 )
-                if (m + 1) % store_tiles == 0:
-                    ms = slice(m + 1 - store_tiles, m + 1)
-                    nc.sync.dma_start(out=out_view[:, ms, cols], in_=res[b][:, ms, cols])
+                nc.sync.dma_start(out=out_view[:, m, :], in_=res[b][:, m, :])
+
+        def project(b, out_tiles):
+            for m in out_tiles:
+                for g in range(GROUPS):
+                    multiply(b, range(m, m + 1), g)
+                finish(b, range(m, m + 1))
 
         all_heads = range(GROUP_HEADS)
         first_half = slice(0, POSITIONS // 2)
@@ -317,8 +325,8 @@ def tile_axialattentionblock_pb_kernel(
         deviations(0, all_t)
         bank_stats(1, all_t[:1])
         divisors(0, all_t)
-        bank_stats(1, all_t[1:2])
         factors(0, all_t)
+        bank_stats(1, all_t[1:2])
         scale_unit(0, all_t)
         sum_unit(2)
         bank_stats(1, all_t[2:])
@@ -332,6 +340,7 @@ def tile_axialattentionblock_pb_kernel(
         bank_stats(2, all_t)
         deviations(2, all_t)
         quantise_unit(0)
+        multiply(0, all_tiles[:4], 0)
         regroup_unit(s_copy, 1, first_half)
         regroup_on_gpsimd(1, second_half)
         divisors(2, all_t)
@@ -345,18 +354,24 @@ def tile_axialattentionblock_pb_kernel(
         regroup_unit(s_copy, 2, first_half)
         regroup_unit(s_copy, 2, second_half)
         divisors(3, all_t)
-        project(0, all_tiles[:1])
+        multiply(0, all_tiles[:4], 1)
+        finish(0, all_tiles[:1])
         factors(3, all_t)
         scale_unit(3, all_t)
-        project(0, all_tiles[1:4])
+        finish(0, all_tiles[1:4])
         quantise_unit(2)
-        project(0, all_tiles[4:6])
+        project(0, all_tiles[4:7])
         regroup_unit(s_copy, 3, first_half)
         regroup_unit(v_copy, 3, second_half)
         for m in all_tiles:
             nc.scalar.activation(
                 out=x_bias[1][:, m, :], in_=x_sb[1][:, m, :], func=ACT.Identity, bias=gamma_bias[:, m : m + 1]
             )
+        for g in range(GROUPS):
+            multiply(0, all_tiles[7:], g)
+        multiply(1, all_tiles[:7], 0)
         quantise_unit(3)
-        project(0, all_tiles[6:])
-        project(1, all_tiles)
+        finish(0, all_tiles[7:])
+        multiply(1, all_tiles[:7], 1)
+        finish(1, all_tiles[:7])
+        project(1, all_tiles[7:])

from contextlib import ExitStack

import concourse.mybir as mybir
from concourse.masks import make_identity

F32 = mybir.dt.float32
BF16 = mybir.dt.bfloat16
I32 = mybir.dt.int32
U32 = mybir.dt.uint32
U8 = mybir.dt.uint8
FP8X4 = mybir.dt.float8_e4m3fn_x4
ACT = mybir.ActivationFunctionType
ALU = mybir.AluOpType

P = 128
PACK = 4
K_PASS = P * PACK
BATCH = 2
HEADS = 8
HEAD_CH = 128
CHANNELS = HEADS * HEAD_CH
POSITIONS = 512
GROUPS = CHANNELS // K_PASS
GROUP_HEADS = K_PASS // HEAD_CH
POS_PER_PART = POSITIONS // P
HEAD_PARTS = HEAD_CH // PACK
OUT_TILES = CHANNELS // P
SCALE_ROWS = 4
EPS = 1e-8
LOAD_HEADS = 2
VECTOR_UNIT = 0
SORTED_UNITS = (1,)
PAIR_POS = P // 2
PAIR_RUNS = POSITIONS // PAIR_POS

FLOPS = 2 * BATCH * CHANNELS * CHANNELS * POSITIONS


def tile_axialattentionblock_pb_kernel(
    tc, xx, xy, x, norm2_w, out_w_words, out_w_scales, out_b, gamma_att, out
):
    nc = tc.nc
    units = [(b, g) for b in range(BATCH) for g in range(GROUPS)]

    with ExitStack() as ctx:
        consts = ctx.enter_context(tc.tile_pool(name="consts", bufs=1))
        per_unit = ctx.enter_context(tc.tile_pool(name="per_unit", bufs=len(units)))
        streams = ctx.enter_context(tc.tile_pool(name="streams", bufs=1))
        per_batch = ctx.enter_context(tc.tile_pool(name="per_batch", bufs=BATCH))
        psum = ctx.enter_context(tc.psum_pool(name="psum", bufs=8))
        ctx.enter_context(tc.manual_schedule())

        ident = consts.tile([P, P], F32)
        make_identity(nc, ident[:])
        ident_bf = consts.tile([P, P], BF16)
        make_identity(nc, ident_bf[:])
        pair_sum = consts.tile([P, PAIR_POS], BF16)
        nc.gpsimd.tensor_tensor(out=pair_sum[:], in0=ident_bf[:, 0:P:2], in1=ident_bf[:, 1:P:2], op=ALU.add)

        w_planes = consts.tile([P, GROUPS, CHANNELS], U8, align_bytes=64)
        nc.vector.memset(w_planes[:].bitcast(I32), 0)

        vec_rows = consts.tile([P, P], BF16)
        nc.vector.memset(vec_rows[:], 0.0)
        nc.scalar.dma_start(out=vec_rows[0:OUT_TILES, :], in_=gamma_att.rearrange("(m p) -> m p", p=P))
        nc.scalar.dma_start(out=vec_rows[OUT_TILES : 2 * OUT_TILES, :], in_=out_b.rearrange("(m p) -> m p", p=P))
        norm_w = consts.tile([P, GROUPS, PACK], BF16)
        nc.scalar.dma_start(out=norm_w[:], in_=norm2_w.rearrange("(g p t) -> p g t", g=GROUPS, t=PACK))

        one = consts.tile([P, 1], F32)
        nc.vector.memset(one[:], 1.0)
        warm = consts.tile([P, 1], F32)
        nc.scalar.activation(out=warm[:], in_=one[:], func=ACT.Sqrt)

        xx_sb = []
        xy_sb = []
        pair_sb = []
        raw_sb = {}
        for u, (b, g) in enumerate(units):
            if u in SORTED_UNITS:
                raw = streams.tile([P, GROUP_HEADS, PAIR_RUNS * HEAD_CH], BF16, name="raw_%d" % u)
                raw_sb[u] = raw
                for h in range(0, GROUP_HEADS, LOAD_HEADS):
                    for s, stream in enumerate((xx, xy)):
                        first = g * GROUP_HEADS + h
                        nc.sync.dma_start(
                            out=raw[s:P:2, h : h + LOAD_HEADS, :],
                            in_=stream[b, first : first + LOAD_HEADS].rearrange("n y (w j) c -> (y w) n (j c)", j=PAIR_RUNS),
                        )
                pair_sb.append(streams.tile([P, PAIR_RUNS, K_PASS], BF16, name="pair_%d" % u))
                xx_sb.append(None)
                xy_sb.append(None)
                continue
            if u != VECTOR_UNIT:
                pair_u = streams.tile([P, PAIR_RUNS, K_PASS], BF16, name="pair_%d" % u)
                for h in range(GROUP_HEADS):
                    for s, stream in enumerate((xx, xy)):
                        nc.sync.dma_start(
                            out=pair_u[s:P:2, :, h * HEAD_CH : (h + 1) * HEAD_CH],
                            in_=stream[b, g * GROUP_HEADS + h].rearrange("(j y) w c -> (y w) j c", j=PAIR_RUNS),
                        )
                pair_sb.append(pair_u)
                xx_sb.append(None)
                xy_sb.append(None)
                continue
            pair_sb.append(None)
            xx_u = streams.tile([P, GROUP_HEADS, POS_PER_PART * HEAD_CH], BF16)
            xy_u = streams.tile([P, GROUP_HEADS, POS_PER_PART * HEAD_CH], BF16)
            for h in range(0, GROUP_HEADS, LOAD_HEADS):
                for stream, tile_u in ((xx, xx_u), (xy, xy_u)):
                    first = g * GROUP_HEADS + h
                    nc.sync.dma_start(
                        out=tile_u[:, h : h + LOAD_HEADS, :],
                        in_=stream[b, first : first + LOAD_HEADS].rearrange(
                            "n y (w i) c -> (y w) n (i c)", i=POS_PER_PART
                        ),
                    )
            xx_sb.append(xx_u)
            xy_sb.append(xy_u)

        scale_rows = out_w_scales.rearrange("g (q r) o -> r q g o", r=SCALE_ROWS)
        for r in range(SCALE_ROWS):
            nc.sync.dma_start(out=w_planes[r:P:32, :, :].bitcast(I32), in_=scale_rows[r].bitcast(I32))
        w_words = consts.tile([P, GROUPS, CHANNELS], U32, align_bytes=64)
        w_view = out_w_words.rearrange("g p o t -> p g (o t)").bitcast(I32)
        x_sb = [per_batch.tile([P, OUT_TILES, POSITIONS], BF16, name="x_sb") for b in range(BATCH)]
        x_view = [x[b].rearrange("(m p) y w -> p m (y w)", p=P) for b in range(BATCH)]
        halves = (slice(0, OUT_TILES // 2), slice(OUT_TILES // 2, OUT_TILES))
        for half in halves:
            o_cols = slice(half.start * P, half.stop * P)
            nc.sync.dma_start(out=w_words[:, :, o_cols].bitcast(I32), in_=w_view[:, :, o_cols])
            nc.sync.dma_start(out=x_sb[0][:, half, :], in_=x_view[0][:, half, :])
        for half in halves:
            nc.sync.dma_start(out=x_sb[1][:, half, :], in_=x_view[1][:, half, :])

        gamma = consts.tile([P, OUT_TILES], F32)
        bias = consts.tile([P, OUT_TILES], F32)
        gamma_bias = consts.tile([P, OUT_TILES], F32)
        one_over_w = consts.tile([P, GROUPS, PACK], F32)
        x_bias = [per_batch.tile([P, OUT_TILES, POSITIONS], F32, name="x_bias") for b in range(BATCH)]
        summed = consts.tile([P, POS_PER_PART, PACK, P], F32)
        res = [per_batch.tile([P, OUT_TILES, POSITIONS], F32, name="res") for b in range(BATCH)]
        products = [[] for b in range(BATCH)]
        banks = [[] for u in units]
        stats = [per_unit.tile([P, PACK, 6], F32, name="stats") for u in units]
        mean_var = [per_unit.tile([P, PACK, 2], F32, name="mean_var") for u in units]
        std = [per_unit.tile([P, PACK], F32, name="std") for u in units]
        divisor = [per_unit.tile([P, PACK], F32, name="divisor") for u in units]
        factor = [per_unit.tile([P, PACK], F32, name="factor") for u in units]
        planes = [per_unit.tile([P, PACK, POSITIONS], BF16, name="planes") for u in units]
        grouped = [per_unit.tile([P, POSITIONS, PACK], BF16, name="grouped", align_bytes=64) for u in units]
        g_words = [per_unit.tile([P, POSITIONS], U32, name="g_words", align_bytes=64) for u in units]
        g_planes = [per_unit.tile([P, POSITIONS], U8, name="g_planes", align_bytes=64) for u in units]

        vec_cols = psum.tile([P, P], BF16, tag="bank")
        nc.tensor.transpose(vec_cols[:], vec_rows[:], ident_bf[:])

        def spread_vectors():
            nc.scalar.copy(out=gamma[:], in_=vec_cols[:, 0:OUT_TILES])
            nc.scalar.copy(out=bias[:], in_=vec_cols[:, OUT_TILES : 2 * OUT_TILES])
            nc.gpsimd.tensor_tensor(out=gamma_bias[:], in0=gamma[:], in1=bias[:], op=ALU.mult)

        def add_bias_to_residual(b, out_tiles):
            for m in out_tiles:
                nc.gpsimd.tensor_scalar(
                    out=x_bias[b][:, m, :],
                    in0=x_sb[b][:, m, :],
                    scalar1=1.0,
                    scalar2=gamma_bias[:, m : m + 1],
                    op0=ALU.mult,
                    op1=ALU.add,
                )

        def add_streams(engine, u, heads):
            for h in heads:
                engine.tensor_tensor(
                    out=summed[:, :, :, h * HEAD_PARTS : (h + 1) * HEAD_PARTS],
                    in0=xx_sb[u][:, h, :].rearrange("q (i c t) -> q i t c", i=POS_PER_PART, t=PACK),
                    in1=xy_sb[u][:, h, :].rearrange("q (i c t) -> q i t c", i=POS_PER_PART, t=PACK),
                    op=ALU.add,
                )

        def transpose_unit(u):
            for t in range(PACK):
                bank = psum.tile([P, POSITIONS], F32, tag="bank")
                for i in range(POS_PER_PART):
                    nc.tensor.transpose(bank[:, i * P : (i + 1) * P], summed[:, i, t, :], ident[:])
                banks[u].append(bank)

        def g_copy(out, in_):
            nc.gpsimd.tensor_scalar(out=out, in0=in_, scalar1=1.0, scalar2=0.0, op0=ALU.mult, op1=ALU.add)

        def sort_heads(copy, u, heads):
            for h in heads:
                copy(
                    out=pair_sb[u][:, :, h * HEAD_CH : (h + 1) * HEAD_CH],
                    in_=raw_sb[u][:, h, :].rearrange("k (j c) -> k j c", j=PAIR_RUNS),
                )

        def sum_unit(u):
            for t in range(PACK):
                bank = psum.tile([P, POSITIONS], F32, tag="bank")
                for j in range(PAIR_RUNS):
                    nc.tensor.matmul(
                        bank[:, j * PAIR_POS : (j + 1) * PAIR_POS],
                        lhsT=pair_sb[u][:, j, t:K_PASS:PACK],
                        rhs=pair_sum[:],
                        start=True,
                        stop=True,
                    )
                banks[u].append(bank)

        def bank_stats(u, ts):
            for t in ts:
                nc.vector.bn_stats(out=stats[u][:, t, :], in_=banks[u][t][:])

        def deviations(u, ts):
            for t in ts:
                nc.vector.bn_aggr(out=mean_var[u][:, t, :], in_=stats[u][:, t, :])
            cols = slice(ts[0], ts[-1] + 1)
            nc.scalar.activation(
                out=std[u][:, cols], in_=mean_var[u][:, cols, 1], func=ACT.Sqrt, scale=POSITIONS / (POSITIONS - 1)
            )

        def divisors(u, ts):
            g = units[u][1]
            cols = slice(ts[0], ts[-1] + 1)
            nc.vector.scalar_tensor_tensor(
                out=divisor[u][:, cols],
                in0=std[u][:, cols],
                scalar=2.0 * EPS,
                in1=one_over_w[:, g, cols],
                op0=ALU.add,
                op1=ALU.mult,
            )

        def factors(u, ts):
            cols = slice(ts[0], ts[-1] + 1)
            nc.vector.reciprocal(out=factor[u][:, cols], in_=divisor[u][:, cols])

        def scale_unit(u, ts):
            for t in ts:
                to, bank = planes[u][:, t, :], banks[u][t][:]
                if u in SORTED_UNITS:
                    to = to.rearrange("p (r j) -> p r j", j=PAIR_RUNS)
                    bank = bank.rearrange("p (j r) -> p r j", j=PAIR_RUNS)
                if u == VECTOR_UNIT:
                    to = to.rearrange("p (q i) -> p q i", i=POS_PER_PART)
                    bank = bank.rearrange("p (i q) -> p q i", i=POS_PER_PART)
                nc.scalar.activation(
                    out=to,
                    in_=bank,
                    func=ACT.Copy,
                    scale=factor[u][:, t : t + 1],
                )

        def regroup_unit(copy, u, cols):
            copy(
                out=grouped[u][:, cols, :].rearrange("p (c i) t -> p c t i", i=4),
                in_=planes[u][:, :, cols].rearrange("p t (c i) -> p c t i", i=4),
            )

        def regroup_on_gpsimd(u, cols):
            g_copy(out=grouped[u][:, cols, :], in_=planes[u][:, :, cols].rearrange("p t n -> p n t"))

        def quantise_unit(u, cols=slice(0, POSITIONS)):
            nc.vector.quantize_mx(
                out=g_words[u][:, cols].bitcast(FP8X4),
                scales=g_planes[u][:, cols],
                in_=grouped[u][:, cols, :].rearrange("p n t -> p (n t)"),
            )

        def multiply(b, out_tiles, g):
            u = b * GROUPS + g
            for m in out_tiles:
                o_cols = slice(m * P, (m + 1) * P)
                if g == 0:
                    products[b].append(psum.tile([P, POSITIONS], F32, tag="bank", name="product"))
                nc.tensor.matmul_mx(
                    out=products[b][m][:],
                    lhsT=w_words[:, g, o_cols].bitcast(FP8X4),
                    lhsT_scale=w_planes[:, g, o_cols],
                    rhs=g_words[u][:].bitcast(FP8X4),
                    rhs_scale=g_planes[u][:],
                    start=(g == 0),
                    stop=(g == GROUPS - 1),
                )

        def finish(b, out_tiles):
            out_view = out[b].rearrange("(m p) y w -> p m (y w)", p=P)
            for m in out_tiles:
                nc.vector.scalar_tensor_tensor(
                    out=res[b][:, m, :],
                    in0=products[b][m][:],
                    scalar=gamma[:, m : m + 1],
                    in1=x_bias[b][:, m, :],
                    op0=ALU.mult,
                    op1=ALU.add,
                )
                nc.sync.dma_start(out=out_view[:, m, :], in_=res[b][:, m, :])

        def project(b, out_tiles):
            for m in out_tiles:
                for g in range(GROUPS):
                    multiply(b, range(m, m + 1), g)
                finish(b, range(m, m + 1))

        all_heads = range(GROUP_HEADS)
        first_half = slice(0, POSITIONS // 2)
        second_half = slice(POSITIONS // 2, POSITIONS)
        all_tiles = range(OUT_TILES)

        all_t = range(PACK)
        v_copy = nc.vector.tensor_copy
        s_copy = nc.scalar.copy

        spread_vectors()
        add_streams(nc.vector, 0, all_heads)
        transpose_unit(0)
        sort_heads(v_copy, 1, all_heads[:2])
        nc.vector.reciprocal(out=one_over_w[:], in_=norm_w[:])
        sort_heads(v_copy, 1, all_heads[2:])
        sum_unit(1)
        bank_stats(0, all_t)
        deviations(0, all_t)
        bank_stats(1, all_t[:1])
        divisors(0, all_t)
        factors(0, all_t)
        bank_stats(1, all_t[1:2])
        scale_unit(0, all_t)
        sum_unit(2)
        bank_stats(1, all_t[2:])
        deviations(1, all_t)
        regroup_unit(s_copy, 0, first_half)
        regroup_on_gpsimd(0, second_half)
        divisors(1, all_t)
        factors(1, all_t)
        scale_unit(1, all_t)
        sum_unit(3)
        bank_stats(2, all_t)
        deviations(2, all_t)
        quantise_unit(0)
        multiply(0, all_tiles[:4], 0)
        regroup_unit(s_copy, 1, first_half)
        regroup_on_gpsimd(1, second_half)
        divisors(2, all_t)
        bank_stats(3, all_t[:1])
        factors(2, all_t)
        scale_unit(2, all_t)
        bank_stats(3, all_t[1:])
        quantise_unit(1)
        deviations(3, all_t)
        add_bias_to_residual(0, all_tiles)
        regroup_unit(s_copy, 2, first_half)
        regroup_unit(s_copy, 2, second_half)
        divisors(3, all_t)
        multiply(0, all_tiles[:4], 1)
        finish(0, all_tiles[:1])
        factors(3, all_t)
        scale_unit(3, all_t)
        finish(0, all_tiles[1:4])
        quantise_unit(2)
        project(0, all_tiles[4:7])
        regroup_unit(s_copy, 3, first_half)
        regroup_unit(v_copy, 3, second_half)
        for m in all_tiles:
            nc.scalar.activation(
                out=x_bias[1][:, m, :], in_=x_sb[1][:, m, :], func=ACT.Identity, bias=gamma_bias[:, m : m + 1]
            )
        for g in range(GROUPS):
            multiply(0, all_tiles[7:], g)
        multiply(1, all_tiles[:7], 0)
        quantise_unit(3)
        finish(0, all_tiles[7:])
        multiply(1, all_tiles[:7], 1)
        finish(1, all_tiles[:7])
        project(1, all_tiles[7:])
